import numpy as np
import ml_dtypes


def mxq(x, axis, fmt="e4m3"):
    dtype, down = {"e4m3": (ml_dtypes.float8_e4m3fn, 7), "e5m2": (ml_dtypes.float8_e5m2, 14)}[fmt]
    v = np.moveaxis(np.asarray(x, np.float32).astype(ml_dtypes.bfloat16).astype(np.float64), axis, -1)
    blocks = v.reshape(v.shape[:-1] + (-1, 32))
    amax = np.abs(blocks).max(-1, keepdims=True)
    byte = np.maximum(np.where(amax > 0, np.frexp(amax)[1] - 1 + 127, 0) - down, 1)
    scale = np.exp2(byte - 127.0)
    codes = (blocks / scale).astype(np.float32).astype(dtype).astype(np.float64)
    return np.moveaxis((codes * scale).reshape(v.shape), -1, axis)


WIDE = False


def mx_kscale(k):
    if not WIDE:
        return np.ones(k)
    levels = np.array([10, -10, 5, -5, 0])
    a = np.random.permutation(np.resize(levels, k // 512 * 4)).reshape(k // 512, 4)
    idx = np.arange(k)
    return np.exp2(a[idx // 512, idx % 128 // 32])


BF16 = ml_dtypes.bfloat16


def bf(x):
    return np.asarray(x, np.float32).astype(BF16)


def f64(x):
    return np.asarray(x).astype(np.float64)


B, L, N, HID, H, D = 1, 128, 384, 1536, 12, 128


def apply_rope(x, rope):
    xp = x.reshape(x.shape[:-1] + (D // 2, 2))
    rp = rope[:, None].reshape(rope.shape[0], 1, rope.shape[1], D // 2, 2)
    cos, sin = rp[..., 0], rp[..., 1]
    x0, x1 = xp[..., 0], xp[..., 1]
    out = np.stack([x0 * cos - x1 * sin, x1 * cos + x0 * sin], axis=-1)
    return out.reshape(x.shape)


def setup_inputs():
    s = mx_kscale(HID)
    return {"img": bf(np.random.standard_normal((B, N, HID)) * s),
            "rope": bf(np.random.standard_normal((B, N, D))),
            "W_img_qkv": bf(np.random.standard_normal((3 * H * D, HID)) / np.sqrt(HID) / s)}


def reference(img, rope, W_img_qkv):
    y = mxq(f64(img), 2, "e4m3") @ mxq(f64(W_img_qkv), 1, "e4m3").T
    y = y.reshape(B, N, 3, H, D).transpose(2, 0, 3, 1, 4)
    r = f64(rope)
    return apply_rope(y[0], r), apply_rope(y[1], r), y[2]

@@ -1,0 +1,176 @@
+from contextlib import ExitStack
+
+from concourse import mybir
+from concourse.masks import make_identity
+
+F32 = mybir.dt.float32
+BF16 = mybir.dt.bfloat16
+U32 = mybir.dt.uint32
+U8 = mybir.dt.uint8
+FP8X4 = mybir.dt.float8_e4m3fn_x4
+MULT = mybir.AluOpType.mult
+ADD = mybir.AluOpType.add
+
+P = 128
+TOKENS = 384
+HID = 1536
+HEADS = 12
+D = 128
+K_PASS = 512
+PASSES = HID // K_PASS
+WORDS = HID // 2
+TOKEN_TILES = TOKENS // P
+GROUP_HEADS = 4
+GROUP_COLS = GROUP_HEADS * D
+HEAD_GROUPS = HEADS // GROUP_HEADS
+PAIRS = D // 2
+
+FLOPS = 2 * TOKENS * 3 * HEADS * D * HID
+
+
+def tile_jointattention_pa_kernel(tc, img, rope, w_qkv, out_q, out_k, out_v):
+    nc = tc.nc
+    outs = [o.rearrange("b h n d -> (b h) n d") for o in (out_q, out_k, out_v)]
+    groups = [(which, hg) for hg in range(HEAD_GROUPS) for which in range(3)]
+
+    with ExitStack() as stack:
+        const = stack.enter_context(tc.tile_pool(name="const", bufs=1))
+        w_pool = stack.enter_context(tc.tile_pool(name="w_rows", bufs=len(groups)))
+        grouped_pool = stack.enter_context(tc.tile_pool(name="grouped", bufs=4))
+        quant_pool = stack.enter_context(tc.tile_pool(name="quant", bufs=3))
+        rot_pool = stack.enter_context(tc.tile_pool(name="rot", bufs=3))
+        out_pool = stack.enter_context(tc.tile_pool(name="out", bufs=6))
+        flip_psum = stack.enter_context(tc.psum_pool(name="flip", bufs=4))
+        acc_psum = stack.enter_context(tc.psum_pool(name="acc", bufs=4))
+
+        img_sb = const.tile([P, TOKEN_TILES, HID], BF16)
+        nc.sync.dma_start(
+            out=img_sb[:], in_=img.flatten_outer_dims().rearrange("(p a) k -> p a k", a=TOKEN_TILES)
+        )
+        rope_sb = const.tile([P, TOKEN_TILES, D], BF16)
+        nc.scalar.dma_start(
+            out=rope_sb[:], in_=rope.flatten_outer_dims().rearrange("(p a) d -> p a d", a=TOKEN_TILES)
+        )
+        w_rows = []
+        for which, hg in groups:
+            first = which * HEADS * D + hg * GROUP_COLS
+            w_sb = w_pool.tile([P, GROUP_HEADS, HID], BF16, name="w_sb")
+            nc.sync.dma_start(
+                out=w_sb[:], in_=w_qkv[first : first + GROUP_COLS, :].rearrange("(h p) k -> p h k", p=P)
+            )
+            w_rows.append(w_sb)
+
+        ident = const.tile([P, P], F32)
+        make_identity(nc, ident[:])
+
+        rope_pairs = rope_sb[:].rearrange("p a (i e) -> p a i e", e=2)
+        cos_twice = const.tile([P, TOKEN_TILES, D], F32)
+        nc.vector.tensor_copy(
+            out=cos_twice[:].rearrange("p a (i e) -> p a i e", e=2),
+            in_=rope_pairs[:, :, :, 0:1].to_broadcast([P, TOKEN_TILES, PAIRS, 2]),
+        )
+        sin_signed = const.tile([P, 2, TOKEN_TILES, PAIRS], F32)
+        nc.vector.tensor_scalar_mul(out=sin_signed[:, 0], in0=rope_pairs[:, :, :, 1], scalar1=-1.0)
+        nc.vector.tensor_copy(out=sin_signed[:, 1], in_=rope_pairs[:, :, :, 1])
+
+        def k_onto_partitions(row_blocks, g, grouped_words):
+            width = P * len(row_blocks)
+            flipped = flip_psum.tile([P, 2, width], F32, name="flipped")
+            for u in range(2):
+                first_word = (K_PASS // 2) * g + P * u
+                for b, rows in enumerate(row_blocks):
+                    nc.tensor.transpose(
+                        flipped[:, u, b * P : (b + 1) * P],
+                        rows.bitcast(F32)[:, first_word : first_word + P],
+                        ident[:],
+                    )
+            nc.scalar.copy(out=grouped_words, in_=flipped[:].rearrange("p u c -> p c u"))
+
+        def as_words(grouped):
+            return grouped[:].rearrange("p c v -> p (c v)").bitcast(F32).rearrange("p (c u) -> p c u", u=2)
+
+        img_codes = const.tile([P, PASSES, TOKENS], U32, align_bytes=64)
+        img_scales = const.tile([P, PASSES, TOKENS], U8, align_bytes=64)
+        for g in range(PASSES):
+            for a in range(TOKEN_TILES):
+                img_grouped = grouped_pool.tile([P, P, 4], BF16, align_bytes=64, name="img_grouped")
+                k_onto_partitions([img_sb[:, a, :]], g, as_words(img_grouped))
+                nc.vector.quantize_mx(
+                    out=img_codes[:, g, a * P : (a + 1) * P].bitcast(FP8X4),
+                    scales=img_scales[:, g, a * P : (a + 1) * P],
+                    in_=img_grouped[:].rearrange("p c v -> p (c v)"),
+                )
+
+        def quantise_group(n):
+            w_codes = quant_pool.tile([P, PASSES, GROUP_COLS], U32, align_bytes=64, name="w_codes")
+            w_scales = quant_pool.tile([P, PASSES, GROUP_COLS], U8, align_bytes=64, name="w_scales")
+            for g in range(PASSES):
+                w_grouped = grouped_pool.tile([P, GROUP_COLS, 4], BF16, align_bytes=64, name="w_grouped")
+                for h in range(0, GROUP_HEADS, 2):
+                    k_onto_partitions(
+                        [w_rows[n][:, h, :], w_rows[n][:, h + 1, :]],
+                        g,
+                        as_words(w_grouped)[:, h * P : (h + 2) * P, :],
+                    )
+                nc.vector.quantize_mx(
+                    out=w_codes[:, g, :].bitcast(FP8X4),
+                    scales=w_scales[:, g, :],
+                    in_=w_grouped[:].rearrange("p c v -> p (c v)"),
+                )
+            return w_codes, w_scales
+
+        def multiply_group(n, w_codes, w_scales):
+            which, hg = groups[n]
+            out_sb = out_pool.tile([P, GROUP_HEADS, TOKEN_TILES, D], F32, name="out_sb")
+            for a in range(TOKEN_TILES):
+                acc = acc_psum.tile([P, GROUP_COLS], F32, name="acc")
+                for g in range(PASSES):
+                    nc.tensor.matmul_mx(
+                        out=acc[:],
+                        lhsT=img_codes[:, g, a * P : (a + 1) * P].bitcast(FP8X4),
+                        lhsT_scale=img_scales[:, g, a * P : (a + 1) * P],
+                        rhs=w_codes[:, g, :].bitcast(FP8X4),
+                        rhs_scale=w_scales[:, g, :],
+                        start=(g == 0),
+                        stop=(g == PASSES - 1),
+                    )
+                result = out_sb[:, :, a, :]
+                by_head = acc[:].rearrange("p (h d) -> p h d", h=GROUP_HEADS)
+                if which == 2:
+                    nc.scalar.copy(out=result, in_=by_head)
+                    continue
+                by_pair = acc[:].rearrange("p (h i e) -> p h i e", h=GROUP_HEADS, e=2)
+                cross = rot_pool.tile([P, 2, GROUP_HEADS, PAIRS], F32, name="cross")
+                for e in range(2):
+                    nc.vector.tensor_tensor(
+                        out=cross[:, e],
+                        in0=by_pair[:, :, :, 1 - e],
+                        in1=sin_signed[:, e, a, :].unsqueeze(1).to_broadcast([P, GROUP_HEADS, PAIRS]),
+                        op=MULT,
+                    )
+                nc.vector.tensor_tensor(
+                    out=result,
+                    in0=by_head,
+                    in1=cos_twice[:, a, :].unsqueeze(1).to_broadcast([P, GROUP_HEADS, D]),
+                    op=MULT,
+                )
+                result_pairs = result.rearrange("p h (i e) -> p h i e", e=2)
+                nc.vector.tensor_tensor(
+                    out=result_pairs,
+                    in0=result_pairs,
+                    in1=cross[:].rearrange("p e h i -> p h i e"),
+                    op=ADD,
+                )
+            nc.sync.dma_start(
+                out=outs[which][hg * GROUP_HEADS : (hg + 1) * GROUP_HEADS].rearrange(
+                    "h (p a) d -> p h (a d)", a=TOKEN_TILES
+                ),
+                in_=out_sb[:].rearrange("p h a d -> p h (a d)"),
+            )
+
+        ready = quantise_group(0)
+        for n in range(1, len(groups)):
+            following = quantise_group(n)
+            multiply_group(n - 1, ready[0], ready[1])
+            ready = following
+        multiply_group(len(groups) - 1, ready[0], ready[1])

@@ -18,12 +18,12 @@ HEADS = 12
 D = 128
 K_PASS = 512
 PASSES = HID // K_PASS
-WORDS = HID // 2
 TOKEN_TILES = TOKENS // P
 GROUP_HEADS = 4
 GROUP_COLS = GROUP_HEADS * D
 HEAD_GROUPS = HEADS // GROUP_HEADS
 PAIRS = D // 2
+Q_PART, K_PART, V_PART = 0, 1, 2
 
 FLOPS = 2 * TOKENS * 3 * HEADS * D * HID
 
@@ -31,12 +31,13 @@ FLOPS = 2 * TOKENS * 3 * HEADS * D * HID
 def tile_jointattention_pa_kernel(tc, img, rope, w_qkv, out_q, out_k, out_v):
     nc = tc.nc
     outs = [o.rearrange("b h n d -> (b h) n d") for o in (out_q, out_k, out_v)]
-    groups = [(which, hg) for hg in range(HEAD_GROUPS) for which in range(3)]
+    groups = [(part, hg) for hg in range(HEAD_GROUPS) for part in (Q_PART, V_PART, K_PART)]
 
     with ExitStack() as stack:
+        stack.enter_context(tc.manual_schedule())
         const = stack.enter_context(tc.tile_pool(name="const", bufs=1))
-        w_pool = stack.enter_context(tc.tile_pool(name="w_rows", bufs=len(groups)))
-        grouped_pool = stack.enter_context(tc.tile_pool(name="grouped", bufs=4))
+        w_pool = stack.enter_context(tc.tile_pool(name="w_rows", bufs=8))
+        grouped_pool = stack.enter_context(tc.tile_pool(name="grouped", bufs=2 * PASSES))
         quant_pool = stack.enter_context(tc.tile_pool(name="quant", bufs=3))
         rot_pool = stack.enter_context(tc.tile_pool(name="rot", bufs=3))
         out_pool = stack.enter_context(tc.tile_pool(name="out", bufs=6))
@@ -44,34 +45,28 @@ def tile_jointattention_pa_kernel(tc, img, rope, w_qkv, out_q, out_k, out_v):
         acc_psum = stack.enter_context(tc.psum_pool(name="acc", bufs=4))
 
         img_sb = const.tile([P, TOKEN_TILES, HID], BF16)
-        nc.sync.dma_start(
-            out=img_sb[:], in_=img.flatten_outer_dims().rearrange("(p a) k -> p a k", a=TOKEN_TILES)
-        )
+        img_tiles = img.flatten_outer_dims().rearrange("(p a) k -> p a k", a=TOKEN_TILES)
         rope_sb = const.tile([P, TOKEN_TILES, D], BF16)
         nc.scalar.dma_start(
             out=rope_sb[:], in_=rope.flatten_outer_dims().rearrange("(p a) d -> p a d", a=TOKEN_TILES)
         )
         w_rows = []
-        for which, hg in groups:
-            first = which * HEADS * D + hg * GROUP_COLS
+        nc.sync.dma_start(out=img_sb[:, 0, :], in_=img_tiles[:, 0, :])
+        for n, (part, hg) in enumerate(groups):
             w_sb = w_pool.tile([P, GROUP_HEADS, HID], BF16, name="w_sb")
-            nc.sync.dma_start(
-                out=w_sb[:], in_=w_qkv[first : first + GROUP_COLS, :].rearrange("(h p) k -> p h k", p=P)
-            )
+            for h in range(0, GROUP_HEADS, 2):
+                first = part * HEADS * D + hg * GROUP_COLS + h * D
+                nc.sync.dma_start(
+                    out=w_sb[:, h : h + 2, :],
+                    in_=w_qkv[first : first + 2 * D, :].rearrange("(h p) k -> p h k", p=P),
+                )
             w_rows.append(w_sb)
+            if n == 0:
+                for a in range(1, TOKEN_TILES):
+                    nc.sync.dma_start(out=img_sb[:, a, :], in_=img_tiles[:, a, :])
 
         ident = const.tile([P, P], F32)
         make_identity(nc, ident[:])
-
-        rope_pairs = rope_sb[:].rearrange("p a (i e) -> p a i e", e=2)
-        cos_twice = const.tile([P, TOKEN_TILES, D], F32)
-        nc.vector.tensor_copy(
-            out=cos_twice[:].rearrange("p a (i e) -> p a i e", e=2),
-            in_=rope_pairs[:, :, :, 0:1].to_broadcast([P, TOKEN_TILES, PAIRS, 2]),
-        )
-        sin_signed = const.tile([P, 2, TOKEN_TILES, PAIRS], F32)
-        nc.vector.tensor_scalar_mul(out=sin_signed[:, 0], in0=rope_pairs[:, :, :, 1], scalar1=-1.0)
-        nc.vector.tensor_copy(out=sin_signed[:, 1], in_=rope_pairs[:, :, :, 1])
 
         def k_onto_partitions(row_blocks, g, grouped_words):
             width = P * len(row_blocks)
@@ -91,8 +86,9 @@ def tile_jointattention_pa_kernel(tc, img, rope, w_qkv, out_q, out_k, out_v):
 
         img_codes = const.tile([P, PASSES, TOKENS], U32, align_bytes=64)
         img_scales = const.tile([P, PASSES, TOKENS], U8, align_bytes=64)
-        for g in range(PASSES):
-            for a in range(TOKEN_TILES):
+
+        def quantise_token_tile(a):
+            for g in range(PASSES):
                 img_grouped = grouped_pool.tile([P, P, 4], BF16, align_bytes=64, name="img_grouped")
                 k_onto_partitions([img_sb[:, a, :]], g, as_words(img_grouped))
                 nc.vector.quantize_mx(
@@ -102,25 +98,29 @@ def tile_jointattention_pa_kernel(tc, img, rope, w_qkv, out_q, out_k, out_v):
                 )
 
         def quantise_group(n):
-            w_codes = quant_pool.tile([P, PASSES, GROUP_COLS], U32, align_bytes=64, name="w_codes")
-            w_scales = quant_pool.tile([P, PASSES, GROUP_COLS], U8, align_bytes=64, name="w_scales")
-            for g in range(PASSES):
-                w_grouped = grouped_pool.tile([P, GROUP_COLS, 4], BF16, align_bytes=64, name="w_grouped")
-                for h in range(0, GROUP_HEADS, 2):
+            w_grouped = [
+                grouped_pool.tile([P, GROUP_COLS, 4], BF16, align_bytes=64, name="w_grouped")
+                for g in range(PASSES)
+            ]
+            for h in range(0, GROUP_HEADS, 2):
+                for g in range(PASSES):
                     k_onto_partitions(
                         [w_rows[n][:, h, :], w_rows[n][:, h + 1, :]],
                         g,
-                        as_words(w_grouped)[:, h * P : (h + 2) * P, :],
+                        as_words(w_grouped[g])[:, h * P : (h + 2) * P, :],
                     )
+            w_codes = quant_pool.tile([P, PASSES, GROUP_COLS], U32, align_bytes=64, name="w_codes")
+            w_scales = quant_pool.tile([P, PASSES, GROUP_COLS], U8, align_bytes=64, name="w_scales")
+            for g in range(PASSES):
                 nc.vector.quantize_mx(
                     out=w_codes[:, g, :].bitcast(FP8X4),
                     scales=w_scales[:, g, :],
-                    in_=w_grouped[:].rearrange("p c v -> p (c v)"),
+                    in_=w_grouped[g][:].rearrange("p c v -> p (c v)"),
                 )
             return w_codes, w_scales
 
         def multiply_group(n, w_codes, w_scales):
-            which, hg = groups[n]
+            part, hg = groups[n]
             out_sb = out_pool.tile([P, GROUP_HEADS, TOKEN_TILES, D], F32, name="out_sb")
             for a in range(TOKEN_TILES):
                 acc = acc_psum.tile([P, GROUP_COLS], F32, name="acc")
@@ -136,7 +136,7 @@ def tile_jointattention_pa_kernel(tc, img, rope, w_qkv, out_q, out_k, out_v):
                     )
                 result = out_sb[:, :, a, :]
                 by_head = acc[:].rearrange("p (h d) -> p h d", h=GROUP_HEADS)
-                if which == 2:
+                if part == V_PART:
                     nc.scalar.copy(out=result, in_=by_head)
                     continue
                 by_pair = acc[:].rearrange("p (h i e) -> p h i e", h=GROUP_HEADS, e=2)
@@ -162,15 +162,31 @@ def tile_jointattention_pa_kernel(tc, img, rope, w_qkv, out_q, out_k, out_v):
                     op=ADD,
                 )
             nc.sync.dma_start(
-                out=outs[which][hg * GROUP_HEADS : (hg + 1) * GROUP_HEADS].rearrange(
+                out=outs[part][hg * GROUP_HEADS : (hg + 1) * GROUP_HEADS].rearrange(
                     "h (p a) d -> p h (a d)", a=TOKEN_TILES
                 ),
                 in_=out_sb[:].rearrange("p h a d -> p h (a d)"),
             )
 
+        quantise_token_tile(0)
         ready = quantise_group(0)
+        for a in range(1, TOKEN_TILES):
+            quantise_token_tile(a)
+
+        rope_pairs = rope_sb[:].rearrange("p a (i e) -> p a i e", e=2)
+        cos_twice = const.tile([P, TOKEN_TILES, D], F32)
+        nc.vector.tensor_copy(
+            out=cos_twice[:].rearrange("p a (i e) -> p a i e", e=2),
+            in_=rope_pairs[:, :, :, 0:1].to_broadcast([P, TOKEN_TILES, PAIRS, 2]),
+        )
+        sin_signed = const.tile([P, 2, TOKEN_TILES, PAIRS], F32)
+        nc.vector.tensor_scalar_mul(out=sin_signed[:, 0], in0=rope_pairs[:, :, :, 1], scalar1=-1.0)
+        nc.vector.tensor_copy(out=sin_signed[:, 1], in_=rope_pairs[:, :, :, 1])
+
+        multiply_group(0, ready[0], ready[1])
+
+        ready = quantise_group(1)
         for n in range(1, len(groups)):
-            following = quantise_group(n)
-            multiply_group(n - 1, ready[0], ready[1])
+            following = quantise_group(n + 1) if n + 1 < len(groups) else None
+            multiply_group(n, ready[0], ready[1])
             ready = following
-        multiply_group(len(groups) - 1, ready[0], ready[1])

@@ -31,16 +31,15 @@ FLOPS = 2 * TOKENS * 3 * HEADS * D * HID
 def tile_jointattention_pa_kernel(tc, img, rope, w_qkv, out_q, out_k, out_v):
     nc = tc.nc
     outs = [o.rearrange("b h n d -> (b h) n d") for o in (out_q, out_k, out_v)]
-    groups = [(part, hg) for hg in range(HEAD_GROUPS) for part in (Q_PART, V_PART, K_PART)]
+    groups = [(part, hg) for hg in range(HEAD_GROUPS) for part in (Q_PART, K_PART, V_PART)]
 
     with ExitStack() as stack:
-        stack.enter_context(tc.manual_schedule())
         const = stack.enter_context(tc.tile_pool(name="const", bufs=1))
         w_pool = stack.enter_context(tc.tile_pool(name="w_rows", bufs=8))
         grouped_pool = stack.enter_context(tc.tile_pool(name="grouped", bufs=2 * PASSES))
         quant_pool = stack.enter_context(tc.tile_pool(name="quant", bufs=3))
-        rot_pool = stack.enter_context(tc.tile_pool(name="rot", bufs=3))
-        out_pool = stack.enter_context(tc.tile_pool(name="out", bufs=6))
+        rot_pool = stack.enter_context(tc.tile_pool(name="rot", bufs=4))
+        out_pool = stack.enter_context(tc.tile_pool(name="out", bufs=8))
         flip_psum = stack.enter_context(tc.psum_pool(name="flip", bufs=4))
         acc_psum = stack.enter_context(tc.psum_pool(name="acc", bufs=4))
 
@@ -155,7 +154,7 @@ def tile_jointattention_pa_kernel(tc, img, rope, w_qkv, out_q, out_k, out_v):
                     op=MULT,
                 )
                 result_pairs = result.rearrange("p h (i e) -> p h i e", e=2)
-                nc.vector.tensor_tensor(
+                nc.gpsimd.tensor_tensor(
                     out=result_pairs,
                     in0=result_pairs,
                     in1=cross[:].rearrange("p e h i -> p h i e"),

from contextlib import ExitStack

from concourse import mybir
from concourse.masks import make_identity

F32 = mybir.dt.float32
BF16 = mybir.dt.bfloat16
U32 = mybir.dt.uint32
U8 = mybir.dt.uint8
FP8X4 = mybir.dt.float8_e4m3fn_x4
MULT = mybir.AluOpType.mult
ADD = mybir.AluOpType.add

P = 128
TOKENS = 384
HID = 1536
HEADS = 12
D = 128
K_PASS = 512
PASSES = HID // K_PASS
TOKEN_TILES = TOKENS // P
GROUP_HEADS = 4
GROUP_COLS = GROUP_HEADS * D
HEAD_GROUPS = HEADS // GROUP_HEADS
PAIRS = D // 2
Q_PART, K_PART, V_PART = 0, 1, 2

FLOPS = 2 * TOKENS * 3 * HEADS * D * HID


def tile_jointattention_pa_kernel(tc, img, rope, w_qkv, out_q, out_k, out_v):
    nc = tc.nc
    outs = [o.rearrange("b h n d -> (b h) n d") for o in (out_q, out_k, out_v)]
    groups = [(part, hg) for hg in range(HEAD_GROUPS) for part in (Q_PART, K_PART, V_PART)]

    with ExitStack() as stack:
        const = stack.enter_context(tc.tile_pool(name="const", bufs=1))
        w_pool = stack.enter_context(tc.tile_pool(name="w_rows", bufs=8))
        grouped_pool = stack.enter_context(tc.tile_pool(name="grouped", bufs=2 * PASSES))
        quant_pool = stack.enter_context(tc.tile_pool(name="quant", bufs=3))
        rot_pool = stack.enter_context(tc.tile_pool(name="rot", bufs=4))
        out_pool = stack.enter_context(tc.tile_pool(name="out", bufs=8))
        flip_psum = stack.enter_context(tc.psum_pool(name="flip", bufs=4))
        acc_psum = stack.enter_context(tc.psum_pool(name="acc", bufs=4))

        img_sb = const.tile([P, TOKEN_TILES, HID], BF16)
        img_tiles = img.flatten_outer_dims().rearrange("(p a) k -> p a k", a=TOKEN_TILES)
        rope_sb = const.tile([P, TOKEN_TILES, D], BF16)
        nc.scalar.dma_start(
            out=rope_sb[:], in_=rope.flatten_outer_dims().rearrange("(p a) d -> p a d", a=TOKEN_TILES)
        )
        w_rows = []
        nc.sync.dma_start(out=img_sb[:, 0, :], in_=img_tiles[:, 0, :])
        for n, (part, hg) in enumerate(groups):
            w_sb = w_pool.tile([P, GROUP_HEADS, HID], BF16, name="w_sb")
            for h in range(0, GROUP_HEADS, 2):
                first = part * HEADS * D + hg * GROUP_COLS + h * D
                nc.sync.dma_start(
                    out=w_sb[:, h : h + 2, :],
                    in_=w_qkv[first : first + 2 * D, :].rearrange("(h p) k -> p h k", p=P),
                )
            w_rows.append(w_sb)
            if n == 0:
                for a in range(1, TOKEN_TILES):
                    nc.sync.dma_start(out=img_sb[:, a, :], in_=img_tiles[:, a, :])

        ident = const.tile([P, P], F32)
        make_identity(nc, ident[:])

        def k_onto_partitions(row_blocks, g, grouped_words):
            width = P * len(row_blocks)
            flipped = flip_psum.tile([P, 2, width], F32, name="flipped")
            for u in range(2):
                first_word = (K_PASS // 2) * g + P * u
                for b, rows in enumerate(row_blocks):
                    nc.tensor.transpose(
                        flipped[:, u, b * P : (b + 1) * P],
                        rows.bitcast(F32)[:, first_word : first_word + P],
                        ident[:],
                    )
            nc.scalar.copy(out=grouped_words, in_=flipped[:].rearrange("p u c -> p c u"))

        def as_words(grouped):
            return grouped[:].rearrange("p c v -> p (c v)").bitcast(F32).rearrange("p (c u) -> p c u", u=2)

        img_codes = const.tile([P, PASSES, TOKENS], U32, align_bytes=64)
        img_scales = const.tile([P, PASSES, TOKENS], U8, align_bytes=64)

        def quantise_token_tile(a):
            for g in range(PASSES):
                img_grouped = grouped_pool.tile([P, P, 4], BF16, align_bytes=64, name="img_grouped")
                k_onto_partitions([img_sb[:, a, :]], g, as_words(img_grouped))
                nc.vector.quantize_mx(
                    out=img_codes[:, g, a * P : (a + 1) * P].bitcast(FP8X4),
                    scales=img_scales[:, g, a * P : (a + 1) * P],
                    in_=img_grouped[:].rearrange("p c v -> p (c v)"),
                )

        def quantise_group(n):
            w_grouped = [
                grouped_pool.tile([P, GROUP_COLS, 4], BF16, align_bytes=64, name="w_grouped")
                for g in range(PASSES)
            ]
            for h in range(0, GROUP_HEADS, 2):
                for g in range(PASSES):
                    k_onto_partitions(
                        [w_rows[n][:, h, :], w_rows[n][:, h + 1, :]],
                        g,
                        as_words(w_grouped[g])[:, h * P : (h + 2) * P, :],
                    )
            w_codes = quant_pool.tile([P, PASSES, GROUP_COLS], U32, align_bytes=64, name="w_codes")
            w_scales = quant_pool.tile([P, PASSES, GROUP_COLS], U8, align_bytes=64, name="w_scales")
            for g in range(PASSES):
                nc.vector.quantize_mx(
                    out=w_codes[:, g, :].bitcast(FP8X4),
                    scales=w_scales[:, g, :],
                    in_=w_grouped[g][:].rearrange("p c v -> p (c v)"),
                )
            return w_codes, w_scales

        def multiply_group(n, w_codes, w_scales):
            part, hg = groups[n]
            out_sb = out_pool.tile([P, GROUP_HEADS, TOKEN_TILES, D], F32, name="out_sb")
            for a in range(TOKEN_TILES):
                acc = acc_psum.tile([P, GROUP_COLS], F32, name="acc")
                for g in range(PASSES):
                    nc.tensor.matmul_mx(
                        out=acc[:],
                        lhsT=img_codes[:, g, a * P : (a + 1) * P].bitcast(FP8X4),
                        lhsT_scale=img_scales[:, g, a * P : (a + 1) * P],
                        rhs=w_codes[:, g, :].bitcast(FP8X4),
                        rhs_scale=w_scales[:, g, :],
                        start=(g == 0),
                        stop=(g == PASSES - 1),
                    )
                result = out_sb[:, :, a, :]
                by_head = acc[:].rearrange("p (h d) -> p h d", h=GROUP_HEADS)
                if part == V_PART:
                    nc.scalar.copy(out=result, in_=by_head)
                    continue
                by_pair = acc[:].rearrange("p (h i e) -> p h i e", h=GROUP_HEADS, e=2)
                cross = rot_pool.tile([P, 2, GROUP_HEADS, PAIRS], F32, name="cross")
                for e in range(2):
                    nc.vector.tensor_tensor(
                        out=cross[:, e],
                        in0=by_pair[:, :, :, 1 - e],
                        in1=sin_signed[:, e, a, :].unsqueeze(1).to_broadcast([P, GROUP_HEADS, PAIRS]),
                        op=MULT,
                    )
                nc.vector.tensor_tensor(
                    out=result,
                    in0=by_head,
                    in1=cos_twice[:, a, :].unsqueeze(1).to_broadcast([P, GROUP_HEADS, D]),
                    op=MULT,
                )
                result_pairs = result.rearrange("p h (i e) -> p h i e", e=2)
                nc.gpsimd.tensor_tensor(
                    out=result_pairs,
                    in0=result_pairs,
                    in1=cross[:].rearrange("p e h i -> p h i e"),
                    op=ADD,
                )
            nc.sync.dma_start(
                out=outs[part][hg * GROUP_HEADS : (hg + 1) * GROUP_HEADS].rearrange(
                    "h (p a) d -> p h (a d)", a=TOKEN_TILES
                ),
                in_=out_sb[:].rearrange("p h a d -> p h (a d)"),
            )

        quantise_token_tile(0)
        ready = quantise_group(0)
        for a in range(1, TOKEN_TILES):
            quantise_token_tile(a)

        rope_pairs = rope_sb[:].rearrange("p a (i e) -> p a i e", e=2)
        cos_twice = const.tile([P, TOKEN_TILES, D], F32)
        nc.vector.tensor_copy(
            out=cos_twice[:].rearrange("p a (i e) -> p a i e", e=2),
            in_=rope_pairs[:, :, :, 0:1].to_broadcast([P, TOKEN_TILES, PAIRS, 2]),
        )
        sin_signed = const.tile([P, 2, TOKEN_TILES, PAIRS], F32)
        nc.vector.tensor_scalar_mul(out=sin_signed[:, 0], in0=rope_pairs[:, :, :, 1], scalar1=-1.0)
        nc.vector.tensor_copy(out=sin_signed[:, 1], in_=rope_pairs[:, :, :, 1])

        multiply_group(0, ready[0], ready[1])

        ready = quantise_group(1)
        for n in range(1, len(groups)):
            following = quantise_group(n + 1) if n + 1 < len(groups) else None
            multiply_group(n, ready[0], ready[1])
            ready = following
